import numpy as np
import ml_dtypes

BF16 = ml_dtypes.bfloat16


def bf(x):
    return np.asarray(x, np.float32).astype(BF16)


def f32(x):
    return np.asarray(x, np.float32)


def f64(x):
    return np.asarray(x).astype(np.float64)


def striped(idx):
    return np.tile(idx.reshape(-1, 16).T, (8, 1))


H, K, M, S, N = 128, 256, 512, 512, 128


def sigmoid(v):
    return 1.0 / (1.0 + np.exp(-v))


def setup_inputs():
    return {
        "base": f32(0.5 * np.random.standard_normal((H, S))),
        "x_in": bf(np.random.standard_normal((K, N))),
        "hidden": bf(np.random.standard_normal((H, N))),
        "cell": f32(np.random.standard_normal((H, N))),
        "w_ih": bf(np.random.standard_normal((K, M)) / np.sqrt(K)),
        "w_hh": bf(np.random.standard_normal((H, M)) / np.sqrt(H)),
        "b": f32(0.5 * np.random.standard_normal((M, 1))),
        "offs": striped(np.random.permutation(S)[:N]),
    }


def reference(base, x_in, hidden, cell, w_ih, w_hh, b, offs):
    idx = offs[:16].T.reshape(-1)
    z = f64(w_ih).T @ f64(x_in) + f64(w_hh).T @ f64(hidden) + f64(b)
    zi, zf, zn, zo = np.split(z, M // H, axis=0)
    c1 = sigmoid(zf) * f64(cell) + sigmoid(zi) * np.tanh(zn)
    out = f64(base).copy()
    out[:, idx] = sigmoid(zo) * np.tanh(c1)
    return out

@@ -1,0 +1,73 @@
+import concourse.mybir as mybir
+
+P = 128
+N = 128
+S = 512
+GATES = 4
+BLOCKS = 3
+
+FLOPS = 2 * BLOCKS * P * GATES * P * N
+
+BF16, F32, U16 = mybir.dt.bfloat16, mybir.dt.float32, mybir.dt.uint16
+MULT, ADD = mybir.AluOpType.mult, mybir.AluOpType.add
+SIGMOID = mybir.ActivationFunctionType.Sigmoid
+TANH = mybir.ActivationFunctionType.Tanh
+
+
+def tile_lstmdecoder_kernel(tc, base, x_in, hidden, cell, w_ih, w_hh, b, offs, out):
+    nc = tc.nc
+    with (
+        tc.tile_pool(name="held", bufs=1) as held,
+        tc.psum_pool(name="psum", bufs=1) as psum,
+    ):
+        offsets = held.tile([P, N // 16], U16, name="offsets")
+        nc.sync.dma_start(offsets[:], offs)
+
+        weight_rows = (w_ih[0:P, :], w_ih[P : 2 * P, :], w_hh)
+        moving_rows = (x_in[0:P, :], x_in[P : 2 * P, :], hidden)
+        weights = [held.tile([P, GATES * P], BF16, name=f"weights{k}") for k in range(BLOCKS)]
+        moving = [held.tile([P, N], BF16, name=f"moving{k}") for k in range(BLOCKS)]
+        for k in range(BLOCKS):
+            nc.scalar.dma_start(moving[k][:], moving_rows[k])
+            nc.sync.dma_start(weights[k][:], weight_rows[k])
+
+        bias = held.tile([P, GATES], F32, name="bias")
+        with nc.allow_non_contiguous_dma(reason="512 floats, one to a partition and gate"):
+            nc.scalar.dma_start(bias[:], b.rearrange("(g c) o -> c (g o)", c=P))
+
+        old_cell = held.tile([P, N], F32, name="old_cell")
+        nc.gpsimd.dma_start(old_cell[:], cell)
+        store = held.tile([P, S], F32, name="store")
+        nc.gpsimd.dma_start(store[:], base)
+
+        z = [psum.tile([P, N], F32, name=f"z{g}") for g in range(GATES)]
+        for k in range(BLOCKS):
+            for g in range(GATES):
+                nc.tensor.matmul(
+                    z[g][:],
+                    weights[k][:, g * P : (g + 1) * P],
+                    moving[k][:],
+                    start=(k == 0),
+                    stop=(k == BLOCKS - 1),
+                )
+
+        gate_input = held.tile([P, N], F32, name="gate_input")
+        gate_forget = held.tile([P, N], F32, name="gate_forget")
+        candidate = held.tile([P, N], F32, name="candidate")
+        gate_output = held.tile([P, N], F32, name="gate_output")
+        nc.scalar.activation(gate_input[:], z[0][:], SIGMOID, bias=bias[:, 0:1])
+        nc.scalar.activation(gate_forget[:], z[1][:], SIGMOID, bias=bias[:, 1:2])
+        nc.scalar.activation(candidate[:], z[2][:], TANH, bias=bias[:, 2:3])
+        nc.scalar.activation(gate_output[:], z[3][:], SIGMOID, bias=bias[:, 3:4])
+
+        kept = held.tile([P, N], F32, name="kept")
+        fresh = held.tile([P, N], F32, name="fresh")
+        new_cell = held.tile([P, N], F32, name="new_cell")
+        nc.vector.tensor_tensor(kept[:], gate_forget[:], old_cell[:], MULT)
+        nc.vector.tensor_tensor(fresh[:], gate_input[:], candidate[:], MULT)
+        nc.vector.tensor_tensor(new_cell[:], kept[:], fresh[:], ADD)
+        squashed = held.tile([P, N], F32, name="squashed")
+        nc.scalar.activation(squashed[:], new_cell[:], TANH)
+
+        nc.vector.tensor_tensor(store[:].indirect(offsets[:]), gate_output[:], squashed[:], MULT)
+        nc.sync.dma_start(out, store[:])

@@ -23,6 +23,10 @@ def tile_lstmdecoder_kernel(tc, base, x_in, hidden, cell, w_ih, w_hh, b, offs, o
         offsets = held.tile([P, N // 16], U16, name="offsets")
         nc.sync.dma_start(offsets[:], offs)
 
+        bias = held.tile([P, GATES], F32, name="bias")
+        with nc.allow_non_contiguous_dma(reason="512 floats, one to a partition and gate"):
+            nc.scalar.dma_start(bias[:], b.rearrange("(g c) o -> c (g o)", c=P))
+
         weight_rows = (w_ih[0:P, :], w_ih[P : 2 * P, :], w_hh)
         moving_rows = (x_in[0:P, :], x_in[P : 2 * P, :], hidden)
         weights = [held.tile([P, GATES * P], BF16, name=f"weights{k}") for k in range(BLOCKS)]
@@ -31,14 +35,14 @@ def tile_lstmdecoder_kernel(tc, base, x_in, hidden, cell, w_ih, w_hh, b, offs, o
             nc.scalar.dma_start(moving[k][:], moving_rows[k])
             nc.sync.dma_start(weights[k][:], weight_rows[k])
 
-        bias = held.tile([P, GATES], F32, name="bias")
-        with nc.allow_non_contiguous_dma(reason="512 floats, one to a partition and gate"):
-            nc.scalar.dma_start(bias[:], b.rearrange("(g c) o -> c (g o)", c=P))
-
         old_cell = held.tile([P, N], F32, name="old_cell")
-        nc.gpsimd.dma_start(old_cell[:], cell)
+        nc.scalar.dma_start(old_cell[:], cell)
         store = held.tile([P, S], F32, name="store")
-        nc.gpsimd.dma_start(store[:], base)
+        nc.sync.dma_start(store[:], base)
+
+        scratch = held.tile([P, 1], F32, name="scratch")
+        nc.vector.memset(scratch[:], 0.0)
+        nc.scalar.activation(scratch[:], scratch[:], SIGMOID)
 
         z = [psum.tile([P, N], F32, name=f"z{g}") for g in range(GATES)]
         for k in range(BLOCKS):

@@ -20,23 +20,22 @@ def tile_lstmdecoder_kernel(tc, base, x_in, hidden, cell, w_ih, w_hh, b, offs, o
         tc.tile_pool(name="held", bufs=1) as held,
         tc.psum_pool(name="psum", bufs=1) as psum,
     ):
-        offsets = held.tile([P, N // 16], U16, name="offsets")
-        nc.sync.dma_start(offsets[:], offs)
-
-        bias = held.tile([P, GATES], F32, name="bias")
-        with nc.allow_non_contiguous_dma(reason="512 floats, one to a partition and gate"):
-            nc.scalar.dma_start(bias[:], b.rearrange("(g c) o -> c (g o)", c=P))
-
         weight_rows = (w_ih[0:P, :], w_ih[P : 2 * P, :], w_hh)
         moving_rows = (x_in[0:P, :], x_in[P : 2 * P, :], hidden)
         weights = [held.tile([P, GATES * P], BF16, name=f"weights{k}") for k in range(BLOCKS)]
         moving = [held.tile([P, N], BF16, name=f"moving{k}") for k in range(BLOCKS)]
         for k in range(BLOCKS):
-            nc.scalar.dma_start(moving[k][:], moving_rows[k])
             nc.sync.dma_start(weights[k][:], weight_rows[k])
+            nc.scalar.dma_start(moving[k][:], moving_rows[k])
+
+        bias = held.tile([P, GATES], F32, name="bias")
+        with nc.allow_non_contiguous_dma(reason="512 floats, one to a partition and gate"):
+            nc.scalar.dma_start(bias[:], b.rearrange("(g c) o -> c (g o)", c=P))
 
         old_cell = held.tile([P, N], F32, name="old_cell")
-        nc.scalar.dma_start(old_cell[:], cell)
+        nc.sync.dma_start(old_cell[:], cell)
+        offsets = held.tile([P, N // 16], U16, name="offsets")
+        nc.sync.dma_start(offsets[:], offs)
         store = held.tile([P, S], F32, name="store")
         nc.sync.dma_start(store[:], base)
 
@@ -45,15 +44,16 @@ def tile_lstmdecoder_kernel(tc, base, x_in, hidden, cell, w_ih, w_hh, b, offs, o
         nc.scalar.activation(scratch[:], scratch[:], SIGMOID)
 
         z = [psum.tile([P, N], F32, name=f"z{g}") for g in range(GATES)]
-        for k in range(BLOCKS):
-            for g in range(GATES):
-                nc.tensor.matmul(
-                    z[g][:],
-                    weights[k][:, g * P : (g + 1) * P],
-                    moving[k][:],
-                    start=(k == 0),
-                    stop=(k == BLOCKS - 1),
-                )
+        for gates in ((0, 1, 2), (3,)):
+            for k in range(BLOCKS):
+                for g in gates:
+                    nc.tensor.matmul(
+                        z[g][:],
+                        weights[k][:, g * P : (g + 1) * P],
+                        moving[k][:],
+                        start=(k == 0),
+                        stop=(k == BLOCKS - 1),
+                    )
 
         gate_input = held.tile([P, N], F32, name="gate_input")
         gate_forget = held.tile([P, N], F32, name="gate_forget")

@@ -4,7 +4,9 @@ P = 128
 N = 128
 S = 512
 GATES = 4
+CELL_GATES = 3
 BLOCKS = 3
+BANK = 512
 
 FLOPS = 2 * BLOCKS * P * GATES * P * N
 
@@ -22,10 +24,11 @@ def tile_lstmdecoder_kernel(tc, base, x_in, hidden, cell, w_ih, w_hh, b, offs, o
     ):
         weight_rows = (w_ih[0:P, :], w_ih[P : 2 * P, :], w_hh)
         moving_rows = (x_in[0:P, :], x_in[P : 2 * P, :], hidden)
-        weights = [held.tile([P, GATES * P], BF16, name=f"weights{k}") for k in range(BLOCKS)]
+        weights = [held.tile([P, CELL_GATES * P], BF16, name=f"weights{k}") for k in range(BLOCKS)]
+        weights_out = [held.tile([P, P], BF16, name=f"weights_out{k}") for k in range(BLOCKS)]
         moving = [held.tile([P, N], BF16, name=f"moving{k}") for k in range(BLOCKS)]
         for k in range(BLOCKS):
-            nc.sync.dma_start(weights[k][:], weight_rows[k])
+            nc.sync.dma_start(weights[k][:], weight_rows[k][:, 0 : CELL_GATES * P])
             nc.scalar.dma_start(moving[k][:], moving_rows[k])
 
         bias = held.tile([P, GATES], F32, name="bias")
@@ -34,6 +37,8 @@ def tile_lstmdecoder_kernel(tc, base, x_in, hidden, cell, w_ih, w_hh, b, offs, o
 
         old_cell = held.tile([P, N], F32, name="old_cell")
         nc.sync.dma_start(old_cell[:], cell)
+        for k in range(BLOCKS):
+            nc.sync.dma_start(weights_out[k][:], weight_rows[k][:, CELL_GATES * P : GATES * P])
         offsets = held.tile([P, N // 16], U16, name="offsets")
         nc.sync.dma_start(offsets[:], offs)
         store = held.tile([P, S], F32, name="store")
@@ -43,26 +48,33 @@ def tile_lstmdecoder_kernel(tc, base, x_in, hidden, cell, w_ih, w_hh, b, offs, o
         nc.vector.memset(scratch[:], 0.0)
         nc.scalar.activation(scratch[:], scratch[:], SIGMOID)
 
-        z = [psum.tile([P, N], F32, name=f"z{g}") for g in range(GATES)]
-        for gates in ((0, 1, 2), (3,)):
-            for k in range(BLOCKS):
-                for g in gates:
-                    nc.tensor.matmul(
-                        z[g][:],
-                        weights[k][:, g * P : (g + 1) * P],
-                        moving[k][:],
-                        start=(k == 0),
-                        stop=(k == BLOCKS - 1),
-                    )
+        z = [psum.tile([P, BANK], F32, name=f"z{g}") for g in range(GATES)]
+        for k in range(BLOCKS):
+            for g in range(CELL_GATES):
+                nc.tensor.matmul(
+                    z[g][:, 0:N],
+                    weights[k][:, g * P : (g + 1) * P],
+                    moving[k][:],
+                    start=(k == 0),
+                    stop=(k == BLOCKS - 1),
+                )
+        for k in range(BLOCKS):
+            nc.tensor.matmul(
+                z[CELL_GATES][:, 0:N],
+                weights_out[k][:],
+                moving[k][:],
+                start=(k == 0),
+                stop=(k == BLOCKS - 1),
+            )
 
         gate_input = held.tile([P, N], F32, name="gate_input")
         gate_forget = held.tile([P, N], F32, name="gate_forget")
         candidate = held.tile([P, N], F32, name="candidate")
         gate_output = held.tile([P, N], F32, name="gate_output")
-        nc.scalar.activation(gate_input[:], z[0][:], SIGMOID, bias=bias[:, 0:1])
-        nc.scalar.activation(gate_forget[:], z[1][:], SIGMOID, bias=bias[:, 1:2])
-        nc.scalar.activation(candidate[:], z[2][:], TANH, bias=bias[:, 2:3])
-        nc.scalar.activation(gate_output[:], z[3][:], SIGMOID, bias=bias[:, 3:4])
+        nc.scalar.activation(gate_input[:], z[0][:, 0:N], SIGMOID, bias=bias[:, 0:1])
+        nc.scalar.activation(gate_forget[:], z[1][:, 0:N], SIGMOID, bias=bias[:, 1:2])
+        nc.scalar.activation(candidate[:], z[2][:, 0:N], TANH, bias=bias[:, 2:3])
+        nc.scalar.activation(gate_output[:], z[3][:, 0:N], SIGMOID, bias=bias[:, 3:4])
 
         kept = held.tile([P, N], F32, name="kept")
         fresh = held.tile([P, N], F32, name="fresh")

@@ -5,7 +5,9 @@ N = 128
 S = 512
 GATES = 4
 CELL_GATES = 3
+CELL_GATE_ORDER = (1, 0, 2)
 BLOCKS = 3
+OUT_BLOCK_ORDER = (2, 0, 1)
 BANK = 512
 
 FLOPS = 2 * BLOCKS * P * GATES * P * N
@@ -24,11 +26,11 @@ def tile_lstmdecoder_kernel(tc, base, x_in, hidden, cell, w_ih, w_hh, b, offs, o
     ):
         weight_rows = (w_ih[0:P, :], w_ih[P : 2 * P, :], w_hh)
         moving_rows = (x_in[0:P, :], x_in[P : 2 * P, :], hidden)
-        weights = [held.tile([P, CELL_GATES * P], BF16, name=f"weights{k}") for k in range(BLOCKS)]
-        weights_out = [held.tile([P, P], BF16, name=f"weights_out{k}") for k in range(BLOCKS)]
+        loaded_gates = (CELL_GATES, CELL_GATES, GATES)
+        weights = [held.tile([P, loaded_gates[k] * P], BF16, name=f"weights{k}") for k in range(BLOCKS)]
         moving = [held.tile([P, N], BF16, name=f"moving{k}") for k in range(BLOCKS)]
         for k in range(BLOCKS):
-            nc.sync.dma_start(weights[k][:], weight_rows[k][:, 0 : CELL_GATES * P])
+            nc.sync.dma_start(weights[k][:], weight_rows[k][:, 0 : loaded_gates[k] * P])
             nc.scalar.dma_start(moving[k][:], moving_rows[k])
 
         bias = held.tile([P, GATES], F32, name="bias")
@@ -37,12 +39,14 @@ def tile_lstmdecoder_kernel(tc, base, x_in, hidden, cell, w_ih, w_hh, b, offs, o
 
         old_cell = held.tile([P, N], F32, name="old_cell")
         nc.sync.dma_start(old_cell[:], cell)
-        for k in range(BLOCKS):
-            nc.sync.dma_start(weights_out[k][:], weight_rows[k][:, CELL_GATES * P : GATES * P])
-        offsets = held.tile([P, N // 16], U16, name="offsets")
-        nc.sync.dma_start(offsets[:], offs)
+        out_columns = slice(CELL_GATES * P, GATES * P)
+        weights_out_x = held.tile([P, 2, P], BF16, name="weights_out_x")
+        nc.sync.dma_start(weights_out_x[:], w_ih[:, out_columns].rearrange("(k p) c -> p k c", p=P))
+        weights_out = (weights_out_x[:, 0, :], weights_out_x[:, 1, :], weights[2][:, out_columns])
         store = held.tile([P, S], F32, name="store")
         nc.sync.dma_start(store[:], base)
+        offsets = held.tile([P, N // 16], U16, name="offsets")
+        nc.sync.dma_start(offsets[:], offs)
 
         scratch = held.tile([P, 1], F32, name="scratch")
         nc.vector.memset(scratch[:], 0.0)
@@ -50,7 +54,7 @@ def tile_lstmdecoder_kernel(tc, base, x_in, hidden, cell, w_ih, w_hh, b, offs, o
 
         z = [psum.tile([P, BANK], F32, name=f"z{g}") for g in range(GATES)]
         for k in range(BLOCKS):
-            for g in range(CELL_GATES):
+            for g in CELL_GATE_ORDER:
                 nc.tensor.matmul(
                     z[g][:, 0:N],
                     weights[k][:, g * P : (g + 1) * P],
@@ -58,21 +62,21 @@ def tile_lstmdecoder_kernel(tc, base, x_in, hidden, cell, w_ih, w_hh, b, offs, o
                     start=(k == 0),
                     stop=(k == BLOCKS - 1),
                 )
-        for k in range(BLOCKS):
+        for k in OUT_BLOCK_ORDER:
             nc.tensor.matmul(
                 z[CELL_GATES][:, 0:N],
-                weights_out[k][:],
+                weights_out[k],
                 moving[k][:],
-                start=(k == 0),
-                stop=(k == BLOCKS - 1),
+                start=(k == OUT_BLOCK_ORDER[0]),
+                stop=(k == OUT_BLOCK_ORDER[-1]),
             )
 
         gate_input = held.tile([P, N], F32, name="gate_input")
         gate_forget = held.tile([P, N], F32, name="gate_forget")
         candidate = held.tile([P, N], F32, name="candidate")
         gate_output = held.tile([P, N], F32, name="gate_output")
-        nc.scalar.activation(gate_input[:], z[0][:, 0:N], SIGMOID, bias=bias[:, 0:1])
         nc.scalar.activation(gate_forget[:], z[1][:, 0:N], SIGMOID, bias=bias[:, 1:2])
+        nc.scalar.activation(gate_input[:], z[0][:, 0:N], SIGMOID, bias=bias[:, 0:1])
         nc.scalar.activation(candidate[:], z[2][:, 0:N], TANH, bias=bias[:, 2:3])
         nc.scalar.activation(gate_output[:], z[3][:, 0:N], SIGMOID, bias=bias[:, 3:4])
 

@@ -7,7 +7,7 @@ GATES = 4
 CELL_GATES = 3
 CELL_GATE_ORDER = (1, 0, 2)
 BLOCKS = 3
-OUT_BLOCK_ORDER = (2, 0, 1)
+OUT_BLOCK_ORDER = (0, 1, 2)
 BANK = 512
 
 FLOPS = 2 * BLOCKS * P * GATES * P * N
@@ -25,13 +25,14 @@ def tile_lstmdecoder_kernel(tc, base, x_in, hidden, cell, w_ih, w_hh, b, offs, o
         tc.psum_pool(name="psum", bufs=1) as psum,
     ):
         weight_rows = (w_ih[0:P, :], w_ih[P : 2 * P, :], w_hh)
-        moving_rows = (x_in[0:P, :], x_in[P : 2 * P, :], hidden)
         loaded_gates = (CELL_GATES, CELL_GATES, GATES)
         weights = [held.tile([P, loaded_gates[k] * P], BF16, name=f"weights{k}") for k in range(BLOCKS)]
-        moving = [held.tile([P, N], BF16, name=f"moving{k}") for k in range(BLOCKS)]
+        moving_all = held.tile([P, BLOCKS, N], BF16, name="moving_all")
+        moving = [moving_all[:, k, :] for k in range(BLOCKS)]
+        nc.scalar.dma_start(moving_all[:, 0:2, :], x_in.rearrange("(k p) j -> p k j", p=P))
+        nc.scalar.dma_start(moving_all[:, 2, :], hidden)
         for k in range(BLOCKS):
             nc.sync.dma_start(weights[k][:], weight_rows[k][:, 0 : loaded_gates[k] * P])
-            nc.scalar.dma_start(moving[k][:], moving_rows[k])
 
         bias = held.tile([P, GATES], F32, name="bias")
         with nc.allow_non_contiguous_dma(reason="512 floats, one to a partition and gate"):
@@ -58,7 +59,7 @@ def tile_lstmdecoder_kernel(tc, base, x_in, hidden, cell, w_ih, w_hh, b, offs, o
                 nc.tensor.matmul(
                     z[g][:, 0:N],
                     weights[k][:, g * P : (g + 1) * P],
-                    moving[k][:],
+                    moving[k],
                     start=(k == 0),
                     stop=(k == BLOCKS - 1),
                 )
@@ -66,7 +67,7 @@ def tile_lstmdecoder_kernel(tc, base, x_in, hidden, cell, w_ih, w_hh, b, offs, o
             nc.tensor.matmul(
                 z[CELL_GATES][:, 0:N],
                 weights_out[k],
-                moving[k][:],
+                moving[k],
                 start=(k == OUT_BLOCK_ORDER[0]),
                 stop=(k == OUT_BLOCK_ORDER[-1]),
             )

@@ -8,6 +8,7 @@ CELL_GATES = 3
 CELL_GATE_ORDER = (1, 0, 2)
 BLOCKS = 3
 OUT_BLOCK_ORDER = (0, 1, 2)
+BLOCK = 32
 BANK = 512
 
 FLOPS = 2 * BLOCKS * P * GATES * P * N
@@ -34,9 +35,15 @@ def tile_lstmdecoder_kernel(tc, base, x_in, hidden, cell, w_ih, w_hh, b, offs, o
         for k in range(BLOCKS):
             nc.sync.dma_start(weights[k][:], weight_rows[k][:, 0 : loaded_gates[k] * P])
 
-        bias = held.tile([P, GATES], F32, name="bias")
-        with nc.allow_non_contiguous_dma(reason="512 floats, one to a partition and gate"):
-            nc.scalar.dma_start(bias[:], b.rearrange("(g c) o -> c (g o)", c=P))
+        bias_rows = held.tile([P, GATES * BLOCK], F32, name="bias_rows", align_bytes=64)
+        bias_columns = held.tile([P, GATES * BLOCK], F32, name="bias_columns", align_bytes=64)
+        nc.vector.memset(bias_rows[:], 0.0)
+        nc.scalar.dma_start(
+            bias_rows[0:P:BLOCK, :].rearrange("q (g i) -> q g i", i=BLOCK),
+            b.rearrange("(g q i) o -> q g (i o)", q=P // BLOCK, i=BLOCK),
+        )
+        nc.vector.transpose(bias_columns[:], bias_rows[:])
+        bias = [bias_columns[:, g * BLOCK : g * BLOCK + 1] for g in range(GATES)]
 
         old_cell = held.tile([P, N], F32, name="old_cell")
         nc.sync.dma_start(old_cell[:], cell)
@@ -76,10 +83,10 @@ def tile_lstmdecoder_kernel(tc, base, x_in, hidden, cell, w_ih, w_hh, b, offs, o
         gate_forget = held.tile([P, N], F32, name="gate_forget")
         candidate = held.tile([P, N], F32, name="candidate")
         gate_output = held.tile([P, N], F32, name="gate_output")
-        nc.scalar.activation(gate_forget[:], z[1][:, 0:N], SIGMOID, bias=bias[:, 1:2])
-        nc.scalar.activation(gate_input[:], z[0][:, 0:N], SIGMOID, bias=bias[:, 0:1])
-        nc.scalar.activation(candidate[:], z[2][:, 0:N], TANH, bias=bias[:, 2:3])
-        nc.scalar.activation(gate_output[:], z[3][:, 0:N], SIGMOID, bias=bias[:, 3:4])
+        nc.scalar.activation(gate_forget[:], z[1][:, 0:N], SIGMOID, bias=bias[1])
+        nc.scalar.activation(gate_input[:], z[0][:, 0:N], SIGMOID, bias=bias[0])
+        nc.scalar.activation(candidate[:], z[2][:, 0:N], TANH, bias=bias[2])
+        nc.scalar.activation(gate_output[:], z[3][:, 0:N], SIGMOID, bias=bias[3])
 
         kept = held.tile([P, N], F32, name="kept")
         fresh = held.tile([P, N], F32, name="fresh")

@@ -25,12 +25,13 @@ def tile_lstmdecoder_kernel(tc, base, x_in, hidden, cell, w_ih, w_hh, b, offs, o
         tc.tile_pool(name="held", bufs=1) as held,
         tc.psum_pool(name="psum", bufs=1) as psum,
     ):
-        weight_rows = (w_ih[0:P, :], w_ih[P : 2 * P, :], w_hh)
+        w_ih_blocks = w_ih.rearrange("(p k) m -> p k m", k=2)
+        weight_rows = (w_ih_blocks[:, 0, :], w_ih_blocks[:, 1, :], w_hh)
         loaded_gates = (CELL_GATES, CELL_GATES, GATES)
         weights = [held.tile([P, loaded_gates[k] * P], BF16, name=f"weights{k}") for k in range(BLOCKS)]
         moving_all = held.tile([P, BLOCKS, N], BF16, name="moving_all")
         moving = [moving_all[:, k, :] for k in range(BLOCKS)]
-        nc.scalar.dma_start(moving_all[:, 0:2, :], x_in.rearrange("(k p) j -> p k j", p=P))
+        nc.scalar.dma_start(moving_all[:, 0:2, :], x_in.rearrange("(p k) j -> p k j", k=2))
         nc.scalar.dma_start(moving_all[:, 2, :], hidden)
         for k in range(BLOCKS):
             nc.sync.dma_start(weights[k][:], weight_rows[k][:, 0 : loaded_gates[k] * P])
@@ -49,7 +50,7 @@ def tile_lstmdecoder_kernel(tc, base, x_in, hidden, cell, w_ih, w_hh, b, offs, o
         nc.sync.dma_start(old_cell[:], cell)
         out_columns = slice(CELL_GATES * P, GATES * P)
         weights_out_x = held.tile([P, 2, P], BF16, name="weights_out_x")
-        nc.sync.dma_start(weights_out_x[:], w_ih[:, out_columns].rearrange("(k p) c -> p k c", p=P))
+        nc.sync.dma_start(weights_out_x[:], w_ih_blocks[:, :, out_columns])
         weights_out = (weights_out_x[:, 0, :], weights_out_x[:, 1, :], weights[2][:, out_columns])
         store = held.tile([P, S], F32, name="store")
         nc.sync.dma_start(store[:], base)

@@ -7,7 +7,7 @@ GATES = 4
 CELL_GATES = 3
 CELL_GATE_ORDER = (1, 0, 2)
 BLOCKS = 3
-OUT_BLOCK_ORDER = (0, 1, 2)
+OUT_BLOCK_ORDER = (2, 0, 1)
 BLOCK = 32
 BANK = 512
 

import concourse.mybir as mybir

P = 128
N = 128
S = 512
GATES = 4
CELL_GATES = 3
CELL_GATE_ORDER = (1, 0, 2)
BLOCKS = 3
OUT_BLOCK_ORDER = (2, 0, 1)
BLOCK = 32
BANK = 512

FLOPS = 2 * BLOCKS * P * GATES * P * N

BF16, F32, U16 = mybir.dt.bfloat16, mybir.dt.float32, mybir.dt.uint16
MULT, ADD = mybir.AluOpType.mult, mybir.AluOpType.add
SIGMOID = mybir.ActivationFunctionType.Sigmoid
TANH = mybir.ActivationFunctionType.Tanh


def tile_lstmdecoder_kernel(tc, base, x_in, hidden, cell, w_ih, w_hh, b, offs, out):
    nc = tc.nc
    with (
        tc.tile_pool(name="held", bufs=1) as held,
        tc.psum_pool(name="psum", bufs=1) as psum,
    ):
        w_ih_blocks = w_ih.rearrange("(p k) m -> p k m", k=2)
        weight_rows = (w_ih_blocks[:, 0, :], w_ih_blocks[:, 1, :], w_hh)
        loaded_gates = (CELL_GATES, CELL_GATES, GATES)
        weights = [held.tile([P, loaded_gates[k] * P], BF16, name=f"weights{k}") for k in range(BLOCKS)]
        moving_all = held.tile([P, BLOCKS, N], BF16, name="moving_all")
        moving = [moving_all[:, k, :] for k in range(BLOCKS)]
        nc.scalar.dma_start(moving_all[:, 0:2, :], x_in.rearrange("(p k) j -> p k j", k=2))
        nc.scalar.dma_start(moving_all[:, 2, :], hidden)
        for k in range(BLOCKS):
            nc.sync.dma_start(weights[k][:], weight_rows[k][:, 0 : loaded_gates[k] * P])

        bias_rows = held.tile([P, GATES * BLOCK], F32, name="bias_rows", align_bytes=64)
        bias_columns = held.tile([P, GATES * BLOCK], F32, name="bias_columns", align_bytes=64)
        nc.vector.memset(bias_rows[:], 0.0)
        nc.scalar.dma_start(
            bias_rows[0:P:BLOCK, :].rearrange("q (g i) -> q g i", i=BLOCK),
            b.rearrange("(g q i) o -> q g (i o)", q=P // BLOCK, i=BLOCK),
        )
        nc.vector.transpose(bias_columns[:], bias_rows[:])
        bias = [bias_columns[:, g * BLOCK : g * BLOCK + 1] for g in range(GATES)]

        old_cell = held.tile([P, N], F32, name="old_cell")
        nc.sync.dma_start(old_cell[:], cell)
        out_columns = slice(CELL_GATES * P, GATES * P)
        weights_out_x = held.tile([P, 2, P], BF16, name="weights_out_x")
        nc.sync.dma_start(weights_out_x[:], w_ih_blocks[:, :, out_columns])
        weights_out = (weights_out_x[:, 0, :], weights_out_x[:, 1, :], weights[2][:, out_columns])
        store = held.tile([P, S], F32, name="store")
        nc.sync.dma_start(store[:], base)
        offsets = held.tile([P, N // 16], U16, name="offsets")
        nc.sync.dma_start(offsets[:], offs)

        scratch = held.tile([P, 1], F32, name="scratch")
        nc.vector.memset(scratch[:], 0.0)
        nc.scalar.activation(scratch[:], scratch[:], SIGMOID)

        z = [psum.tile([P, BANK], F32, name=f"z{g}") for g in range(GATES)]
        for k in range(BLOCKS):
            for g in CELL_GATE_ORDER:
                nc.tensor.matmul(
                    z[g][:, 0:N],
                    weights[k][:, g * P : (g + 1) * P],
                    moving[k],
                    start=(k == 0),
                    stop=(k == BLOCKS - 1),
                )
        for k in OUT_BLOCK_ORDER:
            nc.tensor.matmul(
                z[CELL_GATES][:, 0:N],
                weights_out[k],
                moving[k],
                start=(k == OUT_BLOCK_ORDER[0]),
                stop=(k == OUT_BLOCK_ORDER[-1]),
            )

        gate_input = held.tile([P, N], F32, name="gate_input")
        gate_forget = held.tile([P, N], F32, name="gate_forget")
        candidate = held.tile([P, N], F32, name="candidate")
        gate_output = held.tile([P, N], F32, name="gate_output")
        nc.scalar.activation(gate_forget[:], z[1][:, 0:N], SIGMOID, bias=bias[1])
        nc.scalar.activation(gate_input[:], z[0][:, 0:N], SIGMOID, bias=bias[0])
        nc.scalar.activation(candidate[:], z[2][:, 0:N], TANH, bias=bias[2])
        nc.scalar.activation(gate_output[:], z[3][:, 0:N], SIGMOID, bias=bias[3])

        kept = held.tile([P, N], F32, name="kept")
        fresh = held.tile([P, N], F32, name="fresh")
        new_cell = held.tile([P, N], F32, name="new_cell")
        nc.vector.tensor_tensor(kept[:], gate_forget[:], old_cell[:], MULT)
        nc.vector.tensor_tensor(fresh[:], gate_input[:], candidate[:], MULT)
        nc.vector.tensor_tensor(new_cell[:], kept[:], fresh[:], ADD)
        squashed = held.tile([P, N], F32, name="squashed")
        nc.scalar.activation(squashed[:], new_cell[:], TANH)

        nc.vector.tensor_tensor(store[:].indirect(offsets[:]), gate_output[:], squashed[:], MULT)
        nc.sync.dma_start(out, store[:])
